import numpy as np
import ml_dtypes


def mxq(x, axis, fmt="e4m3"):
    dtype, down = {"e4m3": (ml_dtypes.float8_e4m3fn, 7), "e5m2": (ml_dtypes.float8_e5m2, 14)}[fmt]
    v = np.moveaxis(np.asarray(x, np.float32).astype(ml_dtypes.bfloat16).astype(np.float64), axis, -1)
    blocks = v.reshape(v.shape[:-1] + (-1, 32))
    amax = np.abs(blocks).max(-1, keepdims=True)
    byte = np.maximum(np.where(amax > 0, np.frexp(amax)[1] - 1 + 127, 0) - down, 1)
    scale = np.exp2(byte - 127.0)
    codes = (blocks / scale).astype(np.float32).astype(dtype).astype(np.float64)
    return np.moveaxis((codes * scale).reshape(v.shape), -1, axis)


WIDE = False


def mx_kscale(k):
    if not WIDE:
        return np.ones(k)
    levels = np.array([20, -20, 10, -10, 0])
    a = np.random.permutation(np.resize(levels, k // 512 * 4)).reshape(k // 512, 4)
    idx = np.arange(k)
    return np.exp2(a[idx // 512, idx % 128 // 32])


BF16 = ml_dtypes.bfloat16


def bf(x):
    return np.asarray(x, np.float32).astype(BF16)


def f64(x):
    return np.asarray(x).astype(np.float64)


B, T, HP, WP, NH, D, DFF = 16, 8, 2, 4, 16, 512, 2048
HW = HP * WP
N = B * T * HW


def setup_inputs():
    s = mx_kscale(N).reshape(B * T, HW, 1)
    c = np.random.standard_normal((B * T, 1 + HW, D)) * 1.5 / np.sqrt(1 + HW)
    c[:, 0, :] *= 5.0
    c[:, 1:, :] *= s
    x_res = np.random.standard_normal((B, 1 + HW * T, D)) * 1.1
    w = np.random.standard_normal((D, D)) / np.sqrt(D)
    b = 0.1 * np.random.standard_normal(D)
    g = np.random.standard_normal((B, 1 + HW * T, D)) * np.exp2(np.random.randint(-12, 1, (B, 1 + HW * T, 1)))
    g[:, 1:, :] /= s.reshape(B, T, HW, 1).swapaxes(1, 2).reshape(B, HW * T, 1)
    return {"ctx_s": bf(c), "x_res": bf(x_res), "s_out_w": bf(w), "s_out_b": bf(b), "grad_out": bf(g)}


def reference(ctx_s, x_res, s_out_w, s_out_b, grad_out):
    c = f64(ctx_s)
    g = f64(grad_out)
    cp = c[:, 1:, :].reshape(N, D)
    gp = g[:, 1:, :].reshape(B, HW, T, D).swapaxes(1, 2).reshape(N, D)
    dw = mxq(cp, 0, "e4m3").T @ mxq(gp, 0, "e5m2")
    cc = c[:, 0, :].reshape(B, T, D).mean(axis=1)
    return dw + cc.T @ g[:, 0, :]

@@ -1,0 +1,97 @@
+import concourse.mybir as mybir
+
+FLOPS = 2 * 1024 * 512 * 512 + 2 * 16 * 512 * 512
+BYTES = 128 * 9 * 512 * 2 + 16 * 65 * 512 * 2 + 512 * 512 * 4
+
+BF16 = mybir.dt.bfloat16
+F32 = mybir.dt.float32
+U32 = mybir.dt.uint32
+U8 = mybir.dt.uint8
+E4M3X4 = mybir.dt.float8_e4m3fn_x4
+E5M2X4 = mybir.dt.float8_e5m2_x4
+
+P = 128
+PACK = 4
+D = 512
+SAMPLES = 16
+FRAMES = 8
+PATCHES = 8
+PASSES = FRAMES // PACK
+BLOCKS = D // P
+RUN = 4
+VECTOR_COLS = 256
+
+
+def regroup(copy, grouped, raw, cols):
+    copy(
+        out=grouped[:, cols, :].rearrange("p (c i) j -> p c j i", i=RUN),
+        in_=raw[:, :, cols].rearrange("p j (c i) -> p c j i", i=RUN),
+    )
+
+
+def tile_timesformerlayer_pc_s_kernel(tc, ctx_s, x_res, s_out_w, s_out_b, grad_out, out):
+    nc = tc.nc
+    grad_rows = grad_out[:, 1:, :].rearrange("b (p u j) d -> u b p (j d)", p=PATCHES, u=PASSES, j=PACK)
+    ctx_rows = ctx_s[:, 1:, :].rearrange("(b u j) p d -> u j b p d", b=SAMPLES, u=PASSES, j=PACK)
+
+    with tc.tile_pool(name="keep", bufs=1) as keep, tc.psum_pool(name="psum", bufs=1) as psum:
+        grad_raw = [keep.tile([P, PACK, D], BF16, name="grad_raw%d" % u) for u in range(PASSES)]
+        ctx_raw = [keep.tile([P, PACK, D], BF16, name="ctx_raw%d" % u) for u in range(PASSES)]
+        ctx_cls = keep.tile([P, D], BF16, name="ctx_cls")
+        grad_cls = keep.tile([P, D], BF16, name="grad_cls")
+
+        for u in range(PASSES):
+            nc.sync.dma_start(out=grad_raw[u].rearrange("q j d -> q (j d)"), in_=grad_rows[u])
+        nc.sync.dma_start(out=ctx_cls, in_=ctx_s[:, 0, :])
+        nc.sync.dma_start(out=grad_cls, in_=grad_out[:, 0:1, :].to_broadcast([SAMPLES, FRAMES, D]))
+        for u in range(PASSES):
+            for j in range(PACK):
+                nc.sync.dma_start(out=ctx_raw[u][:, j, :], in_=ctx_rows[u, j])
+
+        cls_part = []
+        for m in range(BLOCKS):
+            cls_acc = psum.tile([P, D], F32, name="cls_acc%d" % m)
+            nc.tensor.matmul(out=cls_acc, lhsT=ctx_cls[:, m * P : (m + 1) * P], rhs=grad_cls, start=True, stop=True)
+            cls_sb = keep.tile([P, D], F32, name="cls_sb%d" % m)
+            nc.scalar.activation(out=cls_sb, in_=cls_acc, func=mybir.ActivationFunctionType.Copy, scale=1.0 / FRAMES)
+            cls_part.append(cls_sb)
+
+        vector_cols = slice(0, VECTOR_COLS)
+        scalar_cols = slice(VECTOR_COLS, D)
+
+        grad_codes = []
+        grad_scales = []
+        for u in range(PASSES):
+            grouped = keep.tile([P, D, PACK], BF16, name="grad_grouped%d" % u, align_bytes=64)
+            regroup(nc.vector.tensor_copy, grouped, grad_raw[u], vector_cols)
+            regroup(nc.scalar.copy, grouped, grad_raw[u], scalar_cols)
+            codes = keep.tile([P, D], U32, name="grad_codes%d" % u, align_bytes=64)
+            scales = keep.tile([P, D], U8, name="grad_scales%d" % u, align_bytes=64)
+            nc.vector.quantize_mx(out=codes.bitcast(E5M2X4), scales=scales, in_=grouped.rearrange("p w j -> p (w j)"))
+            grad_codes.append(codes)
+            grad_scales.append(scales)
+
+        acc = [psum.tile([P, D], F32, name="acc%d" % m) for m in range(BLOCKS)]
+        for u in range(PASSES):
+            grouped = keep.tile([P, D, PACK], BF16, name="ctx_grouped%d" % u, align_bytes=64)
+            regroup(nc.vector.tensor_copy, grouped, ctx_raw[u], vector_cols)
+            regroup(nc.scalar.copy, grouped, ctx_raw[u], scalar_cols)
+            codes = keep.tile([P, D], U32, name="ctx_codes%d" % u, align_bytes=64)
+            scales = keep.tile([P, D], U8, name="ctx_scales%d" % u, align_bytes=64)
+            nc.vector.quantize_mx(out=codes.bitcast(E4M3X4), scales=scales, in_=grouped.rearrange("p w j -> p (w j)"))
+            for m in range(BLOCKS):
+                block = slice(m * P, (m + 1) * P)
+                nc.tensor.matmul_mx(
+                    out=acc[m],
+                    lhsT=codes[:, block].bitcast(E4M3X4),
+                    lhsT_scale=scales[:, block],
+                    rhs=grad_codes[u].bitcast(E5M2X4),
+                    rhs_scale=grad_scales[u],
+                    start=(u == 0),
+                    stop=(u == PASSES - 1),
+                )
+
+        for m in range(BLOCKS):
+            result = keep.tile([P, D], F32, name="result%d" % m)
+            nc.vector.tensor_tensor(out=result, in0=acc[m], in1=cls_part[m], op=mybir.AluOpType.add)
+            nc.sync.dma_start(out=out[m * P : (m + 1) * P, :], in_=result)

@@ -19,14 +19,16 @@ PATCHES = 8
 PASSES = FRAMES // PACK
 BLOCKS = D // P
 RUN = 4
-VECTOR_COLS = 256
+VECTOR_COLS = 320
+HALF = D // 2
 
 
-def regroup(copy, grouped, raw, cols):
-    copy(
-        out=grouped[:, cols, :].rearrange("p (c i) j -> p c j i", i=RUN),
-        in_=raw[:, :, cols].rearrange("p j (c i) -> p c j i", i=RUN),
-    )
+def regroup(nc, grouped, raw):
+    for copy, cols in ((nc.vector.tensor_copy, slice(0, VECTOR_COLS)), (nc.scalar.copy, slice(VECTOR_COLS, D))):
+        copy(
+            out=grouped[:, cols, :].rearrange("p (c i) j -> p c j i", i=RUN),
+            in_=raw[:, :, cols].rearrange("p j (c i) -> p c j i", i=RUN),
+        )
 
 
 def tile_timesformerlayer_pc_s_kernel(tc, ctx_s, x_res, s_out_w, s_out_b, grad_out, out):
@@ -40,45 +42,42 @@ def tile_timesformerlayer_pc_s_kernel(tc, ctx_s, x_res, s_out_w, s_out_b, grad_o
         ctx_cls = keep.tile([P, D], BF16, name="ctx_cls")
         grad_cls = keep.tile([P, D], BF16, name="grad_cls")
 
-        for u in range(PASSES):
-            nc.sync.dma_start(out=grad_raw[u].rearrange("q j d -> q (j d)"), in_=grad_rows[u])
-        nc.sync.dma_start(out=ctx_cls, in_=ctx_s[:, 0, :])
-        nc.sync.dma_start(out=grad_cls, in_=grad_out[:, 0:1, :].to_broadcast([SAMPLES, FRAMES, D]))
-        for u in range(PASSES):
+        def load_ctx(u):
             for j in range(PACK):
                 nc.sync.dma_start(out=ctx_raw[u][:, j, :], in_=ctx_rows[u, j])
 
-        cls_part = []
-        for m in range(BLOCKS):
-            cls_acc = psum.tile([P, D], F32, name="cls_acc%d" % m)
-            nc.tensor.matmul(out=cls_acc, lhsT=ctx_cls[:, m * P : (m + 1) * P], rhs=grad_cls, start=True, stop=True)
-            cls_sb = keep.tile([P, D], F32, name="cls_sb%d" % m)
-            nc.scalar.activation(out=cls_sb, in_=cls_acc, func=mybir.ActivationFunctionType.Copy, scale=1.0 / FRAMES)
-            cls_part.append(cls_sb)
+        for u in range(PASSES):
+            nc.sync.dma_start(out=grad_raw[u].rearrange("q j d -> q (j d)"), in_=grad_rows[u])
+        load_ctx(0)
+        nc.sync.dma_start(out=ctx_cls, in_=ctx_s[:, 0, :])
+        nc.sync.dma_start(out=grad_cls, in_=grad_out[:, 0:1, :].to_broadcast([SAMPLES, FRAMES, D]))
+        load_ctx(1)
 
-        vector_cols = slice(0, VECTOR_COLS)
-        scalar_cols = slice(VECTOR_COLS, D)
-
-        grad_codes = []
-        grad_scales = []
+        grad_codes = [keep.tile([P, D], U32, name="grad_codes%d" % u, align_bytes=64) for u in range(PASSES)]
+        grad_scales = [keep.tile([P, D], U8, name="grad_scales%d" % u, align_bytes=64) for u in range(PASSES)]
         for u in range(PASSES):
             grouped = keep.tile([P, D, PACK], BF16, name="grad_grouped%d" % u, align_bytes=64)
-            regroup(nc.vector.tensor_copy, grouped, grad_raw[u], vector_cols)
-            regroup(nc.scalar.copy, grouped, grad_raw[u], scalar_cols)
-            codes = keep.tile([P, D], U32, name="grad_codes%d" % u, align_bytes=64)
-            scales = keep.tile([P, D], U8, name="grad_scales%d" % u, align_bytes=64)
-            nc.vector.quantize_mx(out=codes.bitcast(E5M2X4), scales=scales, in_=grouped.rearrange("p w j -> p (w j)"))
-            grad_codes.append(codes)
-            grad_scales.append(scales)
+            regroup(nc, grouped, grad_raw[u])
+            nc.vector.quantize_mx(
+                out=grad_codes[u].bitcast(E5M2X4), scales=grad_scales[u], in_=grouped.rearrange("p w j -> p (w j)")
+            )
+
+        cls_acc = [psum.tile([P, D], F32, name="cls_acc%d" % m) for m in range(BLOCKS)]
+        for m in range(BLOCKS):
+            nc.tensor.matmul(out=cls_acc[m], lhsT=ctx_cls[:, m * P : (m + 1) * P], rhs=grad_cls, start=True, stop=True)
 
         acc = [psum.tile([P, D], F32, name="acc%d" % m) for m in range(BLOCKS)]
         for u in range(PASSES):
             grouped = keep.tile([P, D, PACK], BF16, name="ctx_grouped%d" % u, align_bytes=64)
-            regroup(nc.vector.tensor_copy, grouped, ctx_raw[u], vector_cols)
-            regroup(nc.scalar.copy, grouped, ctx_raw[u], scalar_cols)
+            regroup(nc, grouped, ctx_raw[u])
             codes = keep.tile([P, D], U32, name="ctx_codes%d" % u, align_bytes=64)
             scales = keep.tile([P, D], U8, name="ctx_scales%d" % u, align_bytes=64)
-            nc.vector.quantize_mx(out=codes.bitcast(E4M3X4), scales=scales, in_=grouped.rearrange("p w j -> p (w j)"))
+            for cols in (slice(0, HALF), slice(HALF, D)):
+                nc.vector.quantize_mx(
+                    out=codes[:, cols].bitcast(E4M3X4),
+                    scales=scales[:, cols],
+                    in_=grouped[:, cols, :].rearrange("p w j -> p (w j)"),
+                )
             for m in range(BLOCKS):
                 block = slice(m * P, (m + 1) * P)
                 nc.tensor.matmul_mx(
@@ -92,6 +91,8 @@ def tile_timesformerlayer_pc_s_kernel(tc, ctx_s, x_res, s_out_w, s_out_b, grad_o
                 )
 
         for m in range(BLOCKS):
+            cls_part = keep.tile([P, D], F32, name="cls_part%d" % m)
+            nc.scalar.activation(out=cls_part, in_=cls_acc[m], func=mybir.ActivationFunctionType.Copy, scale=1.0 / FRAMES)
             result = keep.tile([P, D], F32, name="result%d" % m)
-            nc.vector.tensor_tensor(out=result, in0=acc[m], in1=cls_part[m], op=mybir.AluOpType.add)
+            nc.vector.tensor_tensor(out=result, in0=acc[m], in1=cls_part, op=mybir.AluOpType.add)
             nc.sync.dma_start(out=out[m * P : (m + 1) * P, :], in_=result)

@@ -19,7 +19,7 @@ PATCHES = 8
 PASSES = FRAMES // PACK
 BLOCKS = D // P
 RUN = 4
-VECTOR_COLS = 320
+VECTOR_COLS = 256
 HALF = D // 2
 
 

@@ -19,7 +19,7 @@ PATCHES = 8
 PASSES = FRAMES // PACK
 BLOCKS = D // P
 RUN = 4
-VECTOR_COLS = 256
+VECTOR_COLS = 384
 HALF = D // 2
 
 

@@ -19,16 +19,11 @@ PATCHES = 8
 PASSES = FRAMES // PACK
 BLOCKS = D // P
 RUN = 4
-VECTOR_COLS = 384
 HALF = D // 2
-
-
-def regroup(nc, grouped, raw):
-    for copy, cols in ((nc.vector.tensor_copy, slice(0, VECTOR_COLS)), (nc.scalar.copy, slice(VECTOR_COLS, D))):
-        copy(
-            out=grouped[:, cols, :].rearrange("p (c i) j -> p c j i", i=RUN),
-            in_=raw[:, :, cols].rearrange("p j (c i) -> p c j i", i=RUN),
-        )
+HALVES = (slice(0, HALF), slice(HALF, D))
+BLOCKS_OF_HALF = ((0, 1), (2, 3))
+VECTOR_COLS = 256
+VECTOR_COLS_LAST = 384
 
 
 def tile_timesformerlayer_pc_s_kernel(tc, ctx_s, x_res, s_out_w, s_out_b, grad_out, out):
@@ -36,59 +31,81 @@ def tile_timesformerlayer_pc_s_kernel(tc, ctx_s, x_res, s_out_w, s_out_b, grad_o
     grad_rows = grad_out[:, 1:, :].rearrange("b (p u j) d -> u b p (j d)", p=PATCHES, u=PASSES, j=PACK)
     ctx_rows = ctx_s[:, 1:, :].rearrange("(b u j) p d -> u j b p d", b=SAMPLES, u=PASSES, j=PACK)
 
-    with tc.tile_pool(name="keep", bufs=1) as keep, tc.psum_pool(name="psum", bufs=1) as psum:
-        grad_raw = [keep.tile([P, PACK, D], BF16, name="grad_raw%d" % u) for u in range(PASSES)]
-        ctx_raw = [keep.tile([P, PACK, D], BF16, name="ctx_raw%d" % u) for u in range(PASSES)]
+    with tc.tile_pool(name="keep", bufs=1) as keep, tc.psum_pool(name="psum", bufs=1) as psum, tc.manual_schedule():
+        names = ["grad0", "grad1", "ctx0", "ctx1"]
+        formats = [E5M2X4, E5M2X4, E4M3X4, E4M3X4]
+        last = len(names) - 1
+        raw = [keep.tile([P, PACK, D], BF16, name="raw_" + n) for n in names]
+        grouped = [keep.tile([P, D, PACK], BF16, name="grouped_" + n, align_bytes=64) for n in names]
+        codes = [keep.tile([P, D], U32, name="codes_" + n, align_bytes=64) for n in names]
+        scales = [keep.tile([P, D], U8, name="scales_" + n, align_bytes=64) for n in names]
         ctx_cls = keep.tile([P, D], BF16, name="ctx_cls")
         grad_cls = keep.tile([P, D], BF16, name="grad_cls")
+        cls_acc = [psum.tile([P, D], F32, name="cls_acc%d" % m) for m in range(BLOCKS)]
+        acc = [psum.tile([P, D], F32, name="acc%d" % m) for m in range(BLOCKS)]
 
         def load_ctx(u):
             for j in range(PACK):
-                nc.sync.dma_start(out=ctx_raw[u][:, j, :], in_=ctx_rows[u, j])
+                nc.sync.dma_start(out=raw[PASSES + u][:, j, :], in_=ctx_rows[u, j])
+
+        def load_class():
+            nc.sync.dma_start(out=ctx_cls, in_=ctx_s[:, 0, :])
+            nc.sync.dma_start(out=grad_cls, in_=grad_out[:, 0:1, :].to_broadcast([SAMPLES, FRAMES, D]))
 
         for u in range(PASSES):
-            nc.sync.dma_start(out=grad_raw[u].rearrange("q j d -> q (j d)"), in_=grad_rows[u])
+            nc.sync.dma_start(out=raw[u].rearrange("q j d -> q (j d)"), in_=grad_rows[u])
+        load_class()
         load_ctx(0)
-        nc.sync.dma_start(out=ctx_cls, in_=ctx_s[:, 0, :])
-        nc.sync.dma_start(out=grad_cls, in_=grad_out[:, 0:1, :].to_broadcast([SAMPLES, FRAMES, D]))
         load_ctx(1)
 
-        grad_codes = [keep.tile([P, D], U32, name="grad_codes%d" % u, align_bytes=64) for u in range(PASSES)]
-        grad_scales = [keep.tile([P, D], U8, name="grad_scales%d" % u, align_bytes=64) for u in range(PASSES)]
-        for u in range(PASSES):
-            grouped = keep.tile([P, D, PACK], BF16, name="grad_grouped%d" % u, align_bytes=64)
-            regroup(nc, grouped, grad_raw[u])
+        def regroup(k):
+            split = VECTOR_COLS_LAST if k == last else VECTOR_COLS
+            for copy, cols in ((nc.vector.tensor_copy, slice(0, split)), (nc.scalar.copy, slice(split, D))):
+                copy(
+                    out=grouped[k][:, cols, :].rearrange("p (c i) j -> p c j i", i=RUN),
+                    in_=raw[k][:, :, cols].rearrange("p j (c i) -> p c j i", i=RUN),
+                )
+
+        def quantise(k, half):
+            cols = HALVES[half]
             nc.vector.quantize_mx(
-                out=grad_codes[u].bitcast(E5M2X4), scales=grad_scales[u], in_=grouped.rearrange("p w j -> p (w j)")
+                out=codes[k][:, cols].bitcast(formats[k]),
+                scales=scales[k][:, cols],
+                in_=grouped[k][:, cols, :].rearrange("p w j -> p (w j)"),
             )
 
-        cls_acc = [psum.tile([P, D], F32, name="cls_acc%d" % m) for m in range(BLOCKS)]
+        def mx_pass(u, m):
+            block = slice(m * P, (m + 1) * P)
+            nc.tensor.matmul_mx(
+                out=acc[m],
+                lhsT=codes[PASSES + u][:, block].bitcast(E4M3X4),
+                lhsT_scale=scales[PASSES + u][:, block],
+                rhs=codes[u].bitcast(E5M2X4),
+                rhs_scale=scales[u],
+                start=(u == 0),
+                stop=(u == PASSES - 1),
+            )
+
+        grad0, grad1, ctx0, ctx1 = range(len(names))
+        regroup(grad0)
+        quantise(grad0, 0)
+        regroup(grad1)
+        quantise(grad0, 1)
+        quantise(grad1, 0)
+        regroup(ctx0)
+        quantise(grad1, 1)
+        quantise(ctx0, 0)
+        regroup(ctx1)
+        quantise(ctx1, 0)
+        quantise(ctx0, 1)
+        quantise(ctx1, 1)
+
         for m in range(BLOCKS):
             nc.tensor.matmul(out=cls_acc[m], lhsT=ctx_cls[:, m * P : (m + 1) * P], rhs=grad_cls, start=True, stop=True)
-
-        acc = [psum.tile([P, D], F32, name="acc%d" % m) for m in range(BLOCKS)]
-        for u in range(PASSES):
-            grouped = keep.tile([P, D, PACK], BF16, name="ctx_grouped%d" % u, align_bytes=64)
-            regroup(nc, grouped, ctx_raw[u])
-            codes = keep.tile([P, D], U32, name="ctx_codes%d" % u, align_bytes=64)
-            scales = keep.tile([P, D], U8, name="ctx_scales%d" % u, align_bytes=64)
-            for cols in (slice(0, HALF), slice(HALF, D)):
-                nc.vector.quantize_mx(
-                    out=codes[:, cols].bitcast(E4M3X4),
-                    scales=scales[:, cols],
-                    in_=grouped[:, cols, :].rearrange("p w j -> p (w j)"),
-                )
-            for m in range(BLOCKS):
-                block = slice(m * P, (m + 1) * P)
-                nc.tensor.matmul_mx(
-                    out=acc[m],
-                    lhsT=codes[:, block].bitcast(E4M3X4),
-                    lhsT_scale=scales[:, block],
-                    rhs=grad_codes[u].bitcast(E5M2X4),
-                    rhs_scale=grad_scales[u],
-                    start=(u == 0),
-                    stop=(u == PASSES - 1),
-                )
+        for blocks in BLOCKS_OF_HALF:
+            for u in range(PASSES):
+                for m in blocks:
+                    mx_pass(u, m)
 
         for m in range(BLOCKS):
             cls_part = keep.tile([P, D], F32, name="cls_part%d" % m)

@@ -19,93 +19,77 @@ PATCHES = 8
 PASSES = FRAMES // PACK
 BLOCKS = D // P
 RUN = 4
+VECTOR_COLS = 384
 HALF = D // 2
-HALVES = (slice(0, HALF), slice(HALF, D))
-BLOCKS_OF_HALF = ((0, 1), (2, 3))
-VECTOR_COLS = 256
-VECTOR_COLS_LAST = 384
+
+
+def regroup(nc, grouped, raw):
+    for copy, cols in ((nc.vector.tensor_copy, slice(0, VECTOR_COLS)), (nc.scalar.copy, slice(VECTOR_COLS, D))):
+        copy(
+            out=grouped[:, cols, :].rearrange("p (c i) j -> p c j i", i=RUN),
+            in_=raw[:, :, cols].rearrange("p j (c i) -> p c j i", i=RUN),
+        )
 
 
 def tile_timesformerlayer_pc_s_kernel(tc, ctx_s, x_res, s_out_w, s_out_b, grad_out, out):
     nc = tc.nc
-    grad_rows = grad_out[:, 1:, :].rearrange("b (p u j) d -> u b p (j d)", p=PATCHES, u=PASSES, j=PACK)
+    grad_rows = grad_out[:, 1:, :].rearrange("b (p u j) d -> u j b p d", p=PATCHES, u=PASSES, j=PACK)
     ctx_rows = ctx_s[:, 1:, :].rearrange("(b u j) p d -> u j b p d", b=SAMPLES, u=PASSES, j=PACK)
 
-    with tc.tile_pool(name="keep", bufs=1) as keep, tc.psum_pool(name="psum", bufs=1) as psum, tc.manual_schedule():
-        names = ["grad0", "grad1", "ctx0", "ctx1"]
-        formats = [E5M2X4, E5M2X4, E4M3X4, E4M3X4]
-        last = len(names) - 1
-        raw = [keep.tile([P, PACK, D], BF16, name="raw_" + n) for n in names]
-        grouped = [keep.tile([P, D, PACK], BF16, name="grouped_" + n, align_bytes=64) for n in names]
-        codes = [keep.tile([P, D], U32, name="codes_" + n, align_bytes=64) for n in names]
-        scales = [keep.tile([P, D], U8, name="scales_" + n, align_bytes=64) for n in names]
+    with tc.tile_pool(name="keep", bufs=1) as keep, tc.psum_pool(name="psum", bufs=1) as psum:
+        grad_raw = [keep.tile([P, PACK, D], BF16, name="grad_raw%d" % u) for u in range(PASSES)]
+        ctx_raw = [keep.tile([P, PACK, D], BF16, name="ctx_raw%d" % u) for u in range(PASSES)]
         ctx_cls = keep.tile([P, D], BF16, name="ctx_cls")
         grad_cls = keep.tile([P, D], BF16, name="grad_cls")
-        cls_acc = [psum.tile([P, D], F32, name="cls_acc%d" % m) for m in range(BLOCKS)]
-        acc = [psum.tile([P, D], F32, name="acc%d" % m) for m in range(BLOCKS)]
 
         def load_ctx(u):
             for j in range(PACK):
-                nc.sync.dma_start(out=raw[PASSES + u][:, j, :], in_=ctx_rows[u, j])
-
-        def load_class():
-            nc.sync.dma_start(out=ctx_cls, in_=ctx_s[:, 0, :])
-            nc.sync.dma_start(out=grad_cls, in_=grad_out[:, 0:1, :].to_broadcast([SAMPLES, FRAMES, D]))
+                nc.sync.dma_start(out=ctx_raw[u][:, j, :], in_=ctx_rows[u, j])
 
         for u in range(PASSES):
-            nc.sync.dma_start(out=raw[u].rearrange("q j d -> q (j d)"), in_=grad_rows[u])
-        load_class()
+            for j in range(PACK):
+                nc.sync.dma_start(out=grad_raw[u][:, j, :], in_=grad_rows[u, j])
         load_ctx(0)
+        nc.sync.dma_start(out=ctx_cls, in_=ctx_s[:, 0, :])
+        nc.sync.dma_start(out=grad_cls, in_=grad_out[:, 0:1, :].to_broadcast([SAMPLES, FRAMES, D]))
         load_ctx(1)
 
-        def regroup(k):
-            split = VECTOR_COLS_LAST if k == last else VECTOR_COLS
-            for copy, cols in ((nc.vector.tensor_copy, slice(0, split)), (nc.scalar.copy, slice(split, D))):
-                copy(
-                    out=grouped[k][:, cols, :].rearrange("p (c i) j -> p c j i", i=RUN),
-                    in_=raw[k][:, :, cols].rearrange("p j (c i) -> p c j i", i=RUN),
-                )
-
-        def quantise(k, half):
-            cols = HALVES[half]
+        grad_codes = [keep.tile([P, D], U32, name="grad_codes%d" % u, align_bytes=64) for u in range(PASSES)]
+        grad_scales = [keep.tile([P, D], U8, name="grad_scales%d" % u, align_bytes=64) for u in range(PASSES)]
+        for u in range(PASSES):
+            grouped = keep.tile([P, D, PACK], BF16, name="grad_grouped%d" % u, align_bytes=64)
+            regroup(nc, grouped, grad_raw[u])
             nc.vector.quantize_mx(
-                out=codes[k][:, cols].bitcast(formats[k]),
-                scales=scales[k][:, cols],
-                in_=grouped[k][:, cols, :].rearrange("p w j -> p (w j)"),
+                out=grad_codes[u].bitcast(E5M2X4), scales=grad_scales[u], in_=grouped.rearrange("p w j -> p (w j)")
             )
 
-        def mx_pass(u, m):
-            block = slice(m * P, (m + 1) * P)
-            nc.tensor.matmul_mx(
-                out=acc[m],
-                lhsT=codes[PASSES + u][:, block].bitcast(E4M3X4),
-                lhsT_scale=scales[PASSES + u][:, block],
-                rhs=codes[u].bitcast(E5M2X4),
-                rhs_scale=scales[u],
-                start=(u == 0),
-                stop=(u == PASSES - 1),
-            )
-
-        grad0, grad1, ctx0, ctx1 = range(len(names))
-        regroup(grad0)
-        quantise(grad0, 0)
-        regroup(grad1)
-        quantise(grad0, 1)
-        quantise(grad1, 0)
-        regroup(ctx0)
-        quantise(grad1, 1)
-        quantise(ctx0, 0)
-        regroup(ctx1)
-        quantise(ctx1, 0)
-        quantise(ctx0, 1)
-        quantise(ctx1, 1)
-
+        cls_acc = [psum.tile([P, D], F32, name="cls_acc%d" % m) for m in range(BLOCKS)]
         for m in range(BLOCKS):
             nc.tensor.matmul(out=cls_acc[m], lhsT=ctx_cls[:, m * P : (m + 1) * P], rhs=grad_cls, start=True, stop=True)
-        for blocks in BLOCKS_OF_HALF:
-            for u in range(PASSES):
-                for m in blocks:
-                    mx_pass(u, m)
+
+        acc = [psum.tile([P, D], F32, name="acc%d" % m) for m in range(BLOCKS)]
+        for u in range(PASSES):
+            grouped = keep.tile([P, D, PACK], BF16, name="ctx_grouped%d" % u, align_bytes=64)
+            regroup(nc, grouped, ctx_raw[u])
+            codes = keep.tile([P, D], U32, name="ctx_codes%d" % u, align_bytes=64)
+            scales = keep.tile([P, D], U8, name="ctx_scales%d" % u, align_bytes=64)
+            for cols in (slice(0, HALF), slice(HALF, D)):
+                nc.vector.quantize_mx(
+                    out=codes[:, cols].bitcast(E4M3X4),
+                    scales=scales[:, cols],
+                    in_=grouped[:, cols, :].rearrange("p w j -> p (w j)"),
+                )
+            for m in range(BLOCKS):
+                block = slice(m * P, (m + 1) * P)
+                nc.tensor.matmul_mx(
+                    out=acc[m],
+                    lhsT=codes[:, block].bitcast(E4M3X4),
+                    lhsT_scale=scales[:, block],
+                    rhs=grad_codes[u].bitcast(E5M2X4),
+                    rhs_scale=grad_scales[u],
+                    start=(u == 0),
+                    stop=(u == PASSES - 1),
+                )
 
         for m in range(BLOCKS):
             cls_part = keep.tile([P, D], F32, name="cls_part%d" % m)

@@ -19,16 +19,18 @@ PATCHES = 8
 PASSES = FRAMES // PACK
 BLOCKS = D // P
 RUN = 4
-VECTOR_COLS = 384
 HALF = D // 2
+LO = slice(0, HALF)
+HI = slice(HALF, D)
+VECTOR_COLS = 304
+LAST_VECTOR_COLS = 352
 
 
-def regroup(nc, grouped, raw):
-    for copy, cols in ((nc.vector.tensor_copy, slice(0, VECTOR_COLS)), (nc.scalar.copy, slice(VECTOR_COLS, D))):
-        copy(
-            out=grouped[:, cols, :].rearrange("p (c i) j -> p c j i", i=RUN),
-            in_=raw[:, :, cols].rearrange("p j (c i) -> p c j i", i=RUN),
-        )
+def regroup(copy, grouped, raw, cols):
+    copy(
+        out=grouped[:, cols, :].rearrange("p (c i) j -> p c j i", i=RUN),
+        in_=raw[:, :, cols].rearrange("p j (c i) -> p c j i", i=RUN),
+    )
 
 
 def tile_timesformerlayer_pc_s_kernel(tc, ctx_s, x_res, s_out_w, s_out_b, grad_out, out):
@@ -36,64 +38,102 @@ def tile_timesformerlayer_pc_s_kernel(tc, ctx_s, x_res, s_out_w, s_out_b, grad_o
     grad_rows = grad_out[:, 1:, :].rearrange("b (p u j) d -> u j b p d", p=PATCHES, u=PASSES, j=PACK)
     ctx_rows = ctx_s[:, 1:, :].rearrange("(b u j) p d -> u j b p d", b=SAMPLES, u=PASSES, j=PACK)
 
-    with tc.tile_pool(name="keep", bufs=1) as keep, tc.psum_pool(name="psum", bufs=1) as psum:
+    with tc.tile_pool(name="keep", bufs=1) as keep, tc.psum_pool(name="psum", bufs=1) as psum, tc.manual_schedule():
         grad_raw = [keep.tile([P, PACK, D], BF16, name="grad_raw%d" % u) for u in range(PASSES)]
         ctx_raw = [keep.tile([P, PACK, D], BF16, name="ctx_raw%d" % u) for u in range(PASSES)]
         ctx_cls = keep.tile([P, D], BF16, name="ctx_cls")
         grad_cls = keep.tile([P, D], BF16, name="grad_cls")
-
-        def load_ctx(u):
-            for j in range(PACK):
-                nc.sync.dma_start(out=ctx_raw[u][:, j, :], in_=ctx_rows[u, j])
-
-        for u in range(PASSES):
-            for j in range(PACK):
-                nc.sync.dma_start(out=grad_raw[u][:, j, :], in_=grad_rows[u, j])
-        load_ctx(0)
-        nc.sync.dma_start(out=ctx_cls, in_=ctx_s[:, 0, :])
-        nc.sync.dma_start(out=grad_cls, in_=grad_out[:, 0:1, :].to_broadcast([SAMPLES, FRAMES, D]))
-        load_ctx(1)
-
+        grad_grouped = [keep.tile([P, D, PACK], BF16, name="grad_grouped%d" % u, align_bytes=64) for u in range(PASSES)]
+        ctx_grouped = [keep.tile([P, D, PACK], BF16, name="ctx_grouped%d" % u, align_bytes=64) for u in range(PASSES)]
         grad_codes = [keep.tile([P, D], U32, name="grad_codes%d" % u, align_bytes=64) for u in range(PASSES)]
         grad_scales = [keep.tile([P, D], U8, name="grad_scales%d" % u, align_bytes=64) for u in range(PASSES)]
-        for u in range(PASSES):
-            grouped = keep.tile([P, D, PACK], BF16, name="grad_grouped%d" % u, align_bytes=64)
-            regroup(nc, grouped, grad_raw[u])
+        ctx_codes = [keep.tile([P, D], U32, name="ctx_codes%d" % u, align_bytes=64) for u in range(PASSES)]
+        ctx_scales = [keep.tile([P, D], U8, name="ctx_scales%d" % u, align_bytes=64) for u in range(PASSES)]
+        cls_acc = [psum.tile([P, D], F32, name="cls_acc%d" % m) for m in range(BLOCKS)]
+        acc = [psum.tile([P, D], F32, name="acc%d" % m) for m in range(BLOCKS)]
+        cls_part = [keep.tile([P, D], F32, name="cls_part%d" % m) for m in range(BLOCKS)]
+
+        def load(raw, rows):
+            for j in range(PACK):
+                nc.sync.dma_start(out=raw[:, j, :], in_=rows[j])
+
+        def quantize_grad(u, cols):
             nc.vector.quantize_mx(
-                out=grad_codes[u].bitcast(E5M2X4), scales=grad_scales[u], in_=grouped.rearrange("p w j -> p (w j)")
+                out=grad_codes[u][:, cols].bitcast(E5M2X4),
+                scales=grad_scales[u][:, cols],
+                in_=grad_grouped[u][:, cols, :].rearrange("p w j -> p (w j)"),
             )
 
-        cls_acc = [psum.tile([P, D], F32, name="cls_acc%d" % m) for m in range(BLOCKS)]
+        def quantize_ctx(u, cols):
+            nc.vector.quantize_mx(
+                out=ctx_codes[u][:, cols].bitcast(E4M3X4),
+                scales=ctx_scales[u][:, cols],
+                in_=ctx_grouped[u][:, cols, :].rearrange("p w j -> p (w j)"),
+            )
+
+        def multiply(u, m):
+            block = slice(m * P, (m + 1) * P)
+            nc.tensor.matmul_mx(
+                out=acc[m],
+                lhsT=ctx_codes[u][:, block].bitcast(E4M3X4),
+                lhsT_scale=ctx_scales[u][:, block],
+                rhs=grad_codes[u].bitcast(E5M2X4),
+                rhs_scale=grad_scales[u],
+                start=(u == 0),
+                stop=(u == PASSES - 1),
+            )
+
+        def copy_cls(m):
+            nc.scalar.activation(
+                out=cls_part[m], in_=cls_acc[m], func=mybir.ActivationFunctionType.Copy, scale=1.0 / FRAMES
+            )
+
+        warm_in = keep.tile([P, 1], F32, name="warm_in")
+        warm_out = keep.tile([P, 1], F32, name="warm_out")
+        nc.vector.memset(warm_in, 0.0)
+        nc.scalar.copy(out=warm_out, in_=warm_in)
+
+        load(grad_raw[0], grad_rows[0])
+        load(ctx_raw[0], ctx_rows[0])
+        nc.sync.dma_start(out=ctx_cls, in_=ctx_s[:, 0, :])
+        nc.sync.dma_start(out=grad_cls, in_=grad_out[:, 0:1, :].to_broadcast([SAMPLES, FRAMES, D]))
+        load(grad_raw[1], grad_rows[1])
+        load(ctx_raw[1], ctx_rows[1])
+
+        early_vector = slice(0, VECTOR_COLS)
+        early_scalar = slice(VECTOR_COLS, D)
+        regroup(nc.vector.tensor_copy, grad_grouped[0], grad_raw[0], early_vector)
+        regroup(nc.scalar.copy, grad_grouped[0], grad_raw[0], early_scalar)
+        quantize_grad(0, LO)
+        regroup(nc.vector.tensor_copy, ctx_grouped[0], ctx_raw[0], early_vector)
+        regroup(nc.scalar.copy, ctx_grouped[0], ctx_raw[0], early_scalar)
+        quantize_grad(0, HI)
+        quantize_ctx(0, LO)
         for m in range(BLOCKS):
             nc.tensor.matmul(out=cls_acc[m], lhsT=ctx_cls[:, m * P : (m + 1) * P], rhs=grad_cls, start=True, stop=True)
-
-        acc = [psum.tile([P, D], F32, name="acc%d" % m) for m in range(BLOCKS)]
-        for u in range(PASSES):
-            grouped = keep.tile([P, D, PACK], BF16, name="ctx_grouped%d" % u, align_bytes=64)
-            regroup(nc, grouped, ctx_raw[u])
-            codes = keep.tile([P, D], U32, name="ctx_codes%d" % u, align_bytes=64)
-            scales = keep.tile([P, D], U8, name="ctx_scales%d" % u, align_bytes=64)
-            for cols in (slice(0, HALF), slice(HALF, D)):
-                nc.vector.quantize_mx(
-                    out=codes[:, cols].bitcast(E4M3X4),
-                    scales=scales[:, cols],
-                    in_=grouped[:, cols, :].rearrange("p w j -> p (w j)"),
-                )
-            for m in range(BLOCKS):
-                block = slice(m * P, (m + 1) * P)
-                nc.tensor.matmul_mx(
-                    out=acc[m],
-                    lhsT=codes[:, block].bitcast(E4M3X4),
-                    lhsT_scale=scales[:, block],
-                    rhs=grad_codes[u].bitcast(E5M2X4),
-                    rhs_scale=grad_scales[u],
-                    start=(u == 0),
-                    stop=(u == PASSES - 1),
-                )
+        multiply(0, 0)
+        multiply(0, 1)
+        regroup(nc.vector.tensor_copy, grad_grouped[1], grad_raw[1], early_vector)
+        regroup(nc.scalar.copy, grad_grouped[1], grad_raw[1], early_scalar)
+        quantize_ctx(0, HI)
+        multiply(0, 2)
+        multiply(0, 3)
+        quantize_grad(1, LO)
+        copy_cls(0)
+        regroup(nc.vector.tensor_copy, ctx_grouped[1], ctx_raw[1], LO)
+        regroup(nc.scalar.copy, ctx_grouped[1], ctx_raw[1], slice(LAST_VECTOR_COLS, D))
+        quantize_grad(1, HI)
+        regroup(nc.vector.tensor_copy, ctx_grouped[1], ctx_raw[1], slice(HALF, LAST_VECTOR_COLS))
+        quantize_ctx(1, LO)
+        multiply(1, 0)
+        multiply(1, 1)
+        quantize_ctx(1, HI)
+        multiply(1, 2)
+        multiply(1, 3)
+        for m in range(1, BLOCKS):
+            copy_cls(m)
 
         for m in range(BLOCKS):
-            cls_part = keep.tile([P, D], F32, name="cls_part%d" % m)
-            nc.scalar.activation(out=cls_part, in_=cls_acc[m], func=mybir.ActivationFunctionType.Copy, scale=1.0 / FRAMES)
             result = keep.tile([P, D], F32, name="result%d" % m)
-            nc.vector.tensor_tensor(out=result, in0=acc[m], in1=cls_part, op=mybir.AluOpType.add)
+            nc.vector.tensor_tensor(out=result, in0=acc[m], in1=cls_part[m], op=mybir.AluOpType.add)
             nc.sync.dma_start(out=out[m * P : (m + 1) * P, :], in_=result)

@@ -23,7 +23,7 @@ HALF = D // 2
 LO = slice(0, HALF)
 HI = slice(HALF, D)
 VECTOR_COLS = 304
-LAST_VECTOR_COLS = 352
+LAST_VECTOR_COLS = 320
 
 
 def regroup(copy, grouped, raw, cols):
@@ -95,10 +95,13 @@ def tile_timesformerlayer_pc_s_kernel(tc, ctx_s, x_res, s_out_w, s_out_b, grad_o
 
         load(grad_raw[0], grad_rows[0])
         load(ctx_raw[0], ctx_rows[0])
-        nc.sync.dma_start(out=ctx_cls, in_=ctx_s[:, 0, :])
-        nc.sync.dma_start(out=grad_cls, in_=grad_out[:, 0:1, :].to_broadcast([SAMPLES, FRAMES, D]))
         load(grad_raw[1], grad_rows[1])
         load(ctx_raw[1], ctx_rows[1])
+        nc.sync.dma_start(out=ctx_cls, in_=ctx_s[:, 0, :])
+        nc.sync.dma_start(out=grad_cls, in_=grad_out[:, 0:1, :].to_broadcast([SAMPLES, FRAMES, D]))
+
+        def multiply_cls(m):
+            nc.tensor.matmul(out=cls_acc[m], lhsT=ctx_cls[:, m * P : (m + 1) * P], rhs=grad_cls, start=True, stop=True)
 
         early_vector = slice(0, VECTOR_COLS)
         early_scalar = slice(VECTOR_COLS, D)
@@ -109,28 +112,29 @@ def tile_timesformerlayer_pc_s_kernel(tc, ctx_s, x_res, s_out_w, s_out_b, grad_o
         regroup(nc.scalar.copy, ctx_grouped[0], ctx_raw[0], early_scalar)
         quantize_grad(0, HI)
         quantize_ctx(0, LO)
-        for m in range(BLOCKS):
-            nc.tensor.matmul(out=cls_acc[m], lhsT=ctx_cls[:, m * P : (m + 1) * P], rhs=grad_cls, start=True, stop=True)
         multiply(0, 0)
         multiply(0, 1)
-        regroup(nc.vector.tensor_copy, grad_grouped[1], grad_raw[1], early_vector)
-        regroup(nc.scalar.copy, grad_grouped[1], grad_raw[1], early_scalar)
         quantize_ctx(0, HI)
         multiply(0, 2)
         multiply(0, 3)
+        regroup(nc.vector.tensor_copy, grad_grouped[1], grad_raw[1], early_vector)
+        regroup(nc.scalar.copy, grad_grouped[1], grad_raw[1], early_scalar)
         quantize_grad(1, LO)
-        copy_cls(0)
+        quantize_grad(1, HI)
         regroup(nc.vector.tensor_copy, ctx_grouped[1], ctx_raw[1], LO)
         regroup(nc.scalar.copy, ctx_grouped[1], ctx_raw[1], slice(LAST_VECTOR_COLS, D))
-        quantize_grad(1, HI)
         regroup(nc.vector.tensor_copy, ctx_grouped[1], ctx_raw[1], slice(HALF, LAST_VECTOR_COLS))
         quantize_ctx(1, LO)
-        multiply(1, 0)
-        multiply(1, 1)
         quantize_ctx(1, HI)
+        multiply_cls(0)
+        multiply_cls(1)
+        multiply(1, 0)
+        multiply_cls(2)
+        multiply(1, 1)
+        multiply_cls(3)
         multiply(1, 2)
         multiply(1, 3)
-        for m in range(1, BLOCKS):
+        for m in range(BLOCKS):
             copy_cls(m)
 
         for m in range(BLOCKS):

@@ -18,7 +18,7 @@ FRAMES = 8
 PATCHES = 8
 PASSES = FRAMES // PACK
 BLOCKS = D // P
-RUN = 4
+RUN = 8
 HALF = D // 2
 LO = slice(0, HALF)
 HI = slice(HALF, D)

@@ -23,7 +23,7 @@ HALF = D // 2
 LO = slice(0, HALF)
 HI = slice(HALF, D)
 VECTOR_COLS = 304
-LAST_VECTOR_COLS = 320
+LAST_VECTOR_COLS = 256
 
 
 def regroup(copy, grouped, raw, cols):
@@ -90,6 +90,8 @@ def tile_timesformerlayer_pc_s_kernel(tc, ctx_s, x_res, s_out_w, s_out_b, grad_o
 
         warm_in = keep.tile([P, 1], F32, name="warm_in")
         warm_out = keep.tile([P, 1], F32, name="warm_out")
+        zeros = keep.tile([P, P], F32, name="zeros")
+        nc.gpsimd.memset(zeros, 0.0)
         nc.vector.memset(warm_in, 0.0)
         nc.scalar.copy(out=warm_out, in_=warm_in)
 
@@ -103,29 +105,36 @@ def tile_timesformerlayer_pc_s_kernel(tc, ctx_s, x_res, s_out_w, s_out_b, grad_o
         def multiply_cls(m):
             nc.tensor.matmul(out=cls_acc[m], lhsT=ctx_cls[:, m * P : (m + 1) * P], rhs=grad_cls, start=True, stop=True)
 
-        early_vector = slice(0, VECTOR_COLS)
-        early_scalar = slice(VECTOR_COLS, D)
-        regroup(nc.vector.tensor_copy, grad_grouped[0], grad_raw[0], early_vector)
-        regroup(nc.scalar.copy, grad_grouped[0], grad_raw[0], early_scalar)
+        def keep_clock_up(raw):
+            nc.tensor.matmul(out=cls_acc[3][:, :HALF], lhsT=zeros, rhs=raw[:, PACK - 1, :].bitcast(F32), start=True, stop=True)
+
+        keep_clock_up(grad_raw[0])
+        keep_clock_up(ctx_raw[0])
+
+        def regroup_early(grouped, raw):
+            regroup(nc.vector.tensor_copy, grouped, raw, LO)
+            regroup(nc.vector.tensor_copy, grouped, raw, slice(HALF, VECTOR_COLS))
+            regroup(nc.scalar.copy, grouped, raw, slice(VECTOR_COLS, D))
+
+        regroup_early(grad_grouped[0], grad_raw[0])
         quantize_grad(0, LO)
-        regroup(nc.vector.tensor_copy, ctx_grouped[0], ctx_raw[0], early_vector)
-        regroup(nc.scalar.copy, ctx_grouped[0], ctx_raw[0], early_scalar)
         quantize_grad(0, HI)
+        regroup_early(ctx_grouped[0], ctx_raw[0])
         quantize_ctx(0, LO)
         multiply(0, 0)
         multiply(0, 1)
         quantize_ctx(0, HI)
         multiply(0, 2)
         multiply(0, 3)
-        regroup(nc.vector.tensor_copy, grad_grouped[1], grad_raw[1], early_vector)
-        regroup(nc.scalar.copy, grad_grouped[1], grad_raw[1], early_scalar)
+        regroup_early(grad_grouped[1], grad_raw[1])
         quantize_grad(1, LO)
         quantize_grad(1, HI)
-        regroup(nc.vector.tensor_copy, ctx_grouped[1], ctx_raw[1], LO)
+        blocks = [slice(m * P, (m + 1) * P) for m in range(BLOCKS)]
+        regroup(nc.vector.tensor_copy, ctx_grouped[1], ctx_raw[1], blocks[0])
         regroup(nc.scalar.copy, ctx_grouped[1], ctx_raw[1], slice(LAST_VECTOR_COLS, D))
-        regroup(nc.vector.tensor_copy, ctx_grouped[1], ctx_raw[1], slice(HALF, LAST_VECTOR_COLS))
-        quantize_ctx(1, LO)
-        quantize_ctx(1, HI)
+        regroup(nc.vector.tensor_copy, ctx_grouped[1], ctx_raw[1], blocks[1])
+        for m in range(BLOCKS):
+            quantize_ctx(1, blocks[m])
         multiply_cls(0)
         multiply_cls(1)
         multiply(1, 0)

@@ -1,4 +1,5 @@
 import concourse.mybir as mybir
+from concourse.masks import make_identity
 
 FLOPS = 2 * 1024 * 512 * 512 + 2 * 16 * 512 * 512
 BYTES = 128 * 9 * 512 * 2 + 16 * 65 * 512 * 2 + 512 * 512 * 4
@@ -43,6 +44,9 @@ def tile_timesformerlayer_pc_s_kernel(tc, ctx_s, x_res, s_out_w, s_out_b, grad_o
         ctx_raw = [keep.tile([P, PACK, D], BF16, name="ctx_raw%d" % u) for u in range(PASSES)]
         ctx_cls = keep.tile([P, D], BF16, name="ctx_cls")
         grad_cls = keep.tile([P, D], BF16, name="grad_cls")
+        grad_cls_rows = keep.tile([P, D], BF16, name="grad_cls_rows")
+        identity = keep.tile([P, P], BF16, name="identity")
+        spread = keep.tile([P, P], BF16, name="spread")
         grad_grouped = [keep.tile([P, D, PACK], BF16, name="grad_grouped%d" % u, align_bytes=64) for u in range(PASSES)]
         ctx_grouped = [keep.tile([P, D, PACK], BF16, name="ctx_grouped%d" % u, align_bytes=64) for u in range(PASSES)]
         grad_codes = [keep.tile([P, D], U32, name="grad_codes%d" % u, align_bytes=64) for u in range(PASSES)]
@@ -92,15 +96,21 @@ def tile_timesformerlayer_pc_s_kernel(tc, ctx_s, x_res, s_out_w, s_out_b, grad_o
         warm_out = keep.tile([P, 1], F32, name="warm_out")
         zeros = keep.tile([P, P], F32, name="zeros")
         nc.gpsimd.memset(zeros, 0.0)
+        nc.vector.memset(grad_cls_rows, 0.0)
+        make_identity(nc, identity[:])
+        nc.vector.tensor_copy(
+            out=spread[:].rearrange("p (b t) -> p b t", t=FRAMES),
+            in_=identity[:, :SAMPLES].unsqueeze(2).to_broadcast([P, SAMPLES, FRAMES]),
+        )
         nc.vector.memset(warm_in, 0.0)
         nc.scalar.copy(out=warm_out, in_=warm_in)
 
         load(grad_raw[0], grad_rows[0])
+        nc.sync.dma_start(out=grad_cls_rows[:SAMPLES, :], in_=grad_out[:, 0, :])
         load(ctx_raw[0], ctx_rows[0])
         load(grad_raw[1], grad_rows[1])
         load(ctx_raw[1], ctx_rows[1])
         nc.sync.dma_start(out=ctx_cls, in_=ctx_s[:, 0, :])
-        nc.sync.dma_start(out=grad_cls, in_=grad_out[:, 0:1, :].to_broadcast([SAMPLES, FRAMES, D]))
 
         def multiply_cls(m):
             nc.tensor.matmul(out=cls_acc[m], lhsT=ctx_cls[:, m * P : (m + 1) * P], rhs=grad_cls, start=True, stop=True)
@@ -108,7 +118,8 @@ def tile_timesformerlayer_pc_s_kernel(tc, ctx_s, x_res, s_out_w, s_out_b, grad_o
         def keep_clock_up(raw):
             nc.tensor.matmul(out=cls_acc[3][:, :HALF], lhsT=zeros, rhs=raw[:, PACK - 1, :].bitcast(F32), start=True, stop=True)
 
-        keep_clock_up(grad_raw[0])
+        spread_acc = cls_acc[2].bitcast(BF16)[:, :D]
+        nc.tensor.matmul(out=spread_acc, lhsT=spread, rhs=grad_cls_rows, start=True, stop=True)
         keep_clock_up(ctx_raw[0])
 
         def regroup_early(grouped, raw):
@@ -117,6 +128,7 @@ def tile_timesformerlayer_pc_s_kernel(tc, ctx_s, x_res, s_out_w, s_out_b, grad_o
             regroup(nc.scalar.copy, grouped, raw, slice(VECTOR_COLS, D))
 
         regroup_early(grad_grouped[0], grad_raw[0])
+        nc.scalar.copy(out=grad_cls, in_=spread_acc)
         quantize_grad(0, LO)
         quantize_grad(0, HI)
         regroup_early(ctx_grouped[0], ctx_raw[0])

import concourse.mybir as mybir
from concourse.masks import make_identity

FLOPS = 2 * 1024 * 512 * 512 + 2 * 16 * 512 * 512
BYTES = 128 * 9 * 512 * 2 + 16 * 65 * 512 * 2 + 512 * 512 * 4

BF16 = mybir.dt.bfloat16
F32 = mybir.dt.float32
U32 = mybir.dt.uint32
U8 = mybir.dt.uint8
E4M3X4 = mybir.dt.float8_e4m3fn_x4
E5M2X4 = mybir.dt.float8_e5m2_x4

P = 128
PACK = 4
D = 512
SAMPLES = 16
FRAMES = 8
PATCHES = 8
PASSES = FRAMES // PACK
BLOCKS = D // P
RUN = 8
HALF = D // 2
LO = slice(0, HALF)
HI = slice(HALF, D)
VECTOR_COLS = 304
LAST_VECTOR_COLS = 256


def regroup(copy, grouped, raw, cols):
    copy(
        out=grouped[:, cols, :].rearrange("p (c i) j -> p c j i", i=RUN),
        in_=raw[:, :, cols].rearrange("p j (c i) -> p c j i", i=RUN),
    )


def tile_timesformerlayer_pc_s_kernel(tc, ctx_s, x_res, s_out_w, s_out_b, grad_out, out):
    nc = tc.nc
    grad_rows = grad_out[:, 1:, :].rearrange("b (p u j) d -> u j b p d", p=PATCHES, u=PASSES, j=PACK)
    ctx_rows = ctx_s[:, 1:, :].rearrange("(b u j) p d -> u j b p d", b=SAMPLES, u=PASSES, j=PACK)

    with tc.tile_pool(name="keep", bufs=1) as keep, tc.psum_pool(name="psum", bufs=1) as psum, tc.manual_schedule():
        grad_raw = [keep.tile([P, PACK, D], BF16, name="grad_raw%d" % u) for u in range(PASSES)]
        ctx_raw = [keep.tile([P, PACK, D], BF16, name="ctx_raw%d" % u) for u in range(PASSES)]
        ctx_cls = keep.tile([P, D], BF16, name="ctx_cls")
        grad_cls = keep.tile([P, D], BF16, name="grad_cls")
        grad_cls_rows = keep.tile([P, D], BF16, name="grad_cls_rows")
        identity = keep.tile([P, P], BF16, name="identity")
        spread = keep.tile([P, P], BF16, name="spread")
        grad_grouped = [keep.tile([P, D, PACK], BF16, name="grad_grouped%d" % u, align_bytes=64) for u in range(PASSES)]
        ctx_grouped = [keep.tile([P, D, PACK], BF16, name="ctx_grouped%d" % u, align_bytes=64) for u in range(PASSES)]
        grad_codes = [keep.tile([P, D], U32, name="grad_codes%d" % u, align_bytes=64) for u in range(PASSES)]
        grad_scales = [keep.tile([P, D], U8, name="grad_scales%d" % u, align_bytes=64) for u in range(PASSES)]
        ctx_codes = [keep.tile([P, D], U32, name="ctx_codes%d" % u, align_bytes=64) for u in range(PASSES)]
        ctx_scales = [keep.tile([P, D], U8, name="ctx_scales%d" % u, align_bytes=64) for u in range(PASSES)]
        cls_acc = [psum.tile([P, D], F32, name="cls_acc%d" % m) for m in range(BLOCKS)]
        acc = [psum.tile([P, D], F32, name="acc%d" % m) for m in range(BLOCKS)]
        cls_part = [keep.tile([P, D], F32, name="cls_part%d" % m) for m in range(BLOCKS)]

        def load(raw, rows):
            for j in range(PACK):
                nc.sync.dma_start(out=raw[:, j, :], in_=rows[j])

        def quantize_grad(u, cols):
            nc.vector.quantize_mx(
                out=grad_codes[u][:, cols].bitcast(E5M2X4),
                scales=grad_scales[u][:, cols],
                in_=grad_grouped[u][:, cols, :].rearrange("p w j -> p (w j)"),
            )

        def quantize_ctx(u, cols):
            nc.vector.quantize_mx(
                out=ctx_codes[u][:, cols].bitcast(E4M3X4),
                scales=ctx_scales[u][:, cols],
                in_=ctx_grouped[u][:, cols, :].rearrange("p w j -> p (w j)"),
            )

        def multiply(u, m):
            block = slice(m * P, (m + 1) * P)
            nc.tensor.matmul_mx(
                out=acc[m],
                lhsT=ctx_codes[u][:, block].bitcast(E4M3X4),
                lhsT_scale=ctx_scales[u][:, block],
                rhs=grad_codes[u].bitcast(E5M2X4),
                rhs_scale=grad_scales[u],
                start=(u == 0),
                stop=(u == PASSES - 1),
            )

        def copy_cls(m):
            nc.scalar.activation(
                out=cls_part[m], in_=cls_acc[m], func=mybir.ActivationFunctionType.Copy, scale=1.0 / FRAMES
            )

        warm_in = keep.tile([P, 1], F32, name="warm_in")
        warm_out = keep.tile([P, 1], F32, name="warm_out")
        zeros = keep.tile([P, P], F32, name="zeros")
        nc.gpsimd.memset(zeros, 0.0)
        nc.vector.memset(grad_cls_rows, 0.0)
        make_identity(nc, identity[:])
        nc.vector.tensor_copy(
            out=spread[:].rearrange("p (b t) -> p b t", t=FRAMES),
            in_=identity[:, :SAMPLES].unsqueeze(2).to_broadcast([P, SAMPLES, FRAMES]),
        )
        nc.vector.memset(warm_in, 0.0)
        nc.scalar.copy(out=warm_out, in_=warm_in)

        load(grad_raw[0], grad_rows[0])
        nc.sync.dma_start(out=grad_cls_rows[:SAMPLES, :], in_=grad_out[:, 0, :])
        load(ctx_raw[0], ctx_rows[0])
        load(grad_raw[1], grad_rows[1])
        load(ctx_raw[1], ctx_rows[1])
        nc.sync.dma_start(out=ctx_cls, in_=ctx_s[:, 0, :])

        def multiply_cls(m):
            nc.tensor.matmul(out=cls_acc[m], lhsT=ctx_cls[:, m * P : (m + 1) * P], rhs=grad_cls, start=True, stop=True)

        def keep_clock_up(raw):
            nc.tensor.matmul(out=cls_acc[3][:, :HALF], lhsT=zeros, rhs=raw[:, PACK - 1, :].bitcast(F32), start=True, stop=True)

        spread_acc = cls_acc[2].bitcast(BF16)[:, :D]
        nc.tensor.matmul(out=spread_acc, lhsT=spread, rhs=grad_cls_rows, start=True, stop=True)
        keep_clock_up(ctx_raw[0])

        def regroup_early(grouped, raw):
            regroup(nc.vector.tensor_copy, grouped, raw, LO)
            regroup(nc.vector.tensor_copy, grouped, raw, slice(HALF, VECTOR_COLS))
            regroup(nc.scalar.copy, grouped, raw, slice(VECTOR_COLS, D))

        regroup_early(grad_grouped[0], grad_raw[0])
        nc.scalar.copy(out=grad_cls, in_=spread_acc)
        quantize_grad(0, LO)
        quantize_grad(0, HI)
        regroup_early(ctx_grouped[0], ctx_raw[0])
        quantize_ctx(0, LO)
        multiply(0, 0)
        multiply(0, 1)
        quantize_ctx(0, HI)
        multiply(0, 2)
        multiply(0, 3)
        regroup_early(grad_grouped[1], grad_raw[1])
        quantize_grad(1, LO)
        quantize_grad(1, HI)
        blocks = [slice(m * P, (m + 1) * P) for m in range(BLOCKS)]
        regroup(nc.vector.tensor_copy, ctx_grouped[1], ctx_raw[1], blocks[0])
        regroup(nc.scalar.copy, ctx_grouped[1], ctx_raw[1], slice(LAST_VECTOR_COLS, D))
        regroup(nc.vector.tensor_copy, ctx_grouped[1], ctx_raw[1], blocks[1])
        for m in range(BLOCKS):
            quantize_ctx(1, blocks[m])
        multiply_cls(0)
        multiply_cls(1)
        multiply(1, 0)
        multiply_cls(2)
        multiply(1, 1)
        multiply_cls(3)
        multiply(1, 2)
        multiply(1, 3)
        for m in range(BLOCKS):
            copy_cls(m)

        for m in range(BLOCKS):
            result = keep.tile([P, D], F32, name="result%d" % m)
            nc.vector.tensor_tensor(out=result, in0=acc[m], in1=cls_part[m], op=mybir.AluOpType.add)
            nc.sync.dma_start(out=out[m * P : (m + 1) * P, :], in_=result)
